import numpy as np
import ml_dtypes


def mxq(x, axis, fmt="e4m3"):
    dtype, down = {"e4m3": (ml_dtypes.float8_e4m3fn, 7), "e5m2": (ml_dtypes.float8_e5m2, 14)}[fmt]
    v = np.moveaxis(np.asarray(x, np.float32).astype(ml_dtypes.bfloat16).astype(np.float64), axis, -1)
    blocks = v.reshape(v.shape[:-1] + (-1, 32))
    amax = np.abs(blocks).max(-1, keepdims=True)
    byte = np.maximum(np.where(amax > 0, np.frexp(amax)[1] - 1 + 127, 0) - down, 1)
    scale = np.exp2(byte - 127.0)
    codes = (blocks / scale).astype(np.float32).astype(dtype).astype(np.float64)
    return np.moveaxis((codes * scale).reshape(v.shape), -1, axis)


WIDE = False


def mx_kscale(k):
    if not WIDE:
        return np.ones(k)
    levels = np.array([10, -10, 5, -5, 0])
    a = np.random.permutation(np.resize(levels, k // 512 * 4)).reshape(k // 512, 4)
    idx = np.arange(k)
    return np.exp2(a[idx // 512, idx % 128 // 32])


BF16 = ml_dtypes.bfloat16


def bf(x):
    return np.asarray(x, np.float32).astype(BF16)


def f64(x):
    return np.asarray(x).astype(np.float64)


B, T, D = 1, 1024, 512


def setup_inputs():
    c = mx_kscale(D)
    return {"q": bf(np.random.standard_normal((B, T, D)) * c),
            "k": bf(np.random.standard_normal((B, T, D)) / c),
            "v": bf(np.random.standard_normal((B, T, D))),
            "s": bf(np.random.standard_normal((B, T, D)) * 0.25 * np.sqrt(T))}


def reference(q, k, v, s):
    d_k = q.shape[-1]
    weights = mxq(f64(q), 2, "e4m3") @ mxq(f64(k), 2, "e4m3").transpose(0, 2, 1)
    z = weights / np.sqrt(d_k)
    e = np.exp(z - z.max(-1, keepdims=True))
    uncertainty = (mxq(e, 2, "e4m3") @ mxq(f64(s), 1, "e4m3")) / e.sum(-1, keepdims=True)
    return uncertainty * f64(v)

@@ -1,0 +1,181 @@
+from contextlib import ExitStack
+import math
+
+import concourse.mybir as mybir
+from concourse.masks import make_identity
+
+FLOPS = 2 * 2 * 1024 * 1024 * 512
+
+BF16 = mybir.dt.bfloat16
+F32 = mybir.dt.float32
+U32 = mybir.dt.uint32
+U8 = mybir.dt.uint8
+FP8X4 = mybir.dt.float8_e4m3fn_x4
+ACT = mybir.ActivationFunctionType
+ALU = mybir.AluOpType
+AX = mybir.AxisListType
+
+P = 128
+T = 1024
+D = 512
+NT = T // P
+
+
+def tile_sourceawareattention_kernel(tc, q, k, v, s, out):
+    nc = tc.nc
+    inv_sqrt_d = 1.0 / math.sqrt(D)
+
+    q2 = q.flatten_outer_dims()
+    k2 = k.flatten_outer_dims()
+    v2 = v.flatten_outer_dims()
+    s2 = s.flatten_outer_dims()
+    o2 = out.flatten_outer_dims()
+
+    q_view = q2.rearrange("(p i) d -> p i d", i=NT)
+    v_view = v2.rearrange("(p i) d -> p i d", i=NT)
+    o_view = o2.rearrange("(p i) d -> p i d", i=NT)
+    k_view = k2.rearrange("(c p t) d -> p c t d", c=2, t=4)
+    s_view = s2.rearrange("(c p t) d -> p c t d", c=2, t=4)
+
+    with ExitStack() as ctx:
+        const = ctx.enter_context(tc.tile_pool(name="const", bufs=1))
+        keep = ctx.enter_context(tc.tile_pool(name="keep", bufs=1))
+        work = ctx.enter_context(tc.tile_pool(name="work", bufs=3))
+        small = ctx.enter_context(tc.tile_pool(name="small", bufs=4))
+        psz = ctx.enter_context(tc.psum_pool(name="psz", bufs=4))
+        pst = ctx.enter_context(tc.psum_pool(name="pst", bufs=2))
+        pso = ctx.enter_context(tc.psum_pool(name="pso", bufs=2))
+
+        k_sb = keep.tile([P, 2, 4, D], BF16, name="k_sb")
+        q_sb = keep.tile([P, NT, D], BF16, name="q_sb")
+        s_sb = keep.tile([P, 2, 4, D], BF16, name="s_sb")
+        v_sb = keep.tile([P, NT, D], BF16, name="v_sb")
+        for c in range(2):
+            nc.sync.dma_start(out=k_sb[:, c], in_=k_view[:, c])
+        for h in range(2):
+            nc.sync.dma_start(out=q_sb[:, 4 * h : 4 * h + 4, :], in_=q_view[:, 4 * h : 4 * h + 4, :])
+        for c in range(2):
+            nc.sync.dma_start(out=s_sb[:, c], in_=s_view[:, c])
+        for h in range(2):
+            nc.sync.dma_start(out=v_sb[:, 4 * h : 4 * h + 4, :], in_=v_view[:, 4 * h : 4 * h + 4, :])
+
+        ident_f = const.tile([P, P], F32, name="ident_f")
+        make_identity(nc, ident_f[:])
+        ident_b = const.tile([P, P], BF16, name="ident_b")
+        make_identity(nc, ident_b[:])
+        warm_in = const.tile([P, 1], F32, name="warm_in")
+        warm_out = const.tile([P, 1], F32, name="warm_out")
+        nc.vector.memset(warm_in[:], 0.0)
+        nc.scalar.activation(out=warm_out[:], in_=warm_in[:], func=ACT.Exp)
+
+        kg = keep.tile([P, 4 * T], BF16, name="kg", align_bytes=64)
+        qg = keep.tile([P, 4 * T], BF16, name="qg", align_bytes=64)
+        kc = keep.tile([P, T], U32, name="kc", align_bytes=64)
+        qc = keep.tile([P, T], U32, name="qc", align_bytes=64)
+        ks = keep.tile([P, T], U8, name="ks", align_bytes=64)
+        qs = keep.tile([P, T], U8, name="qs", align_bytes=64)
+
+        def turn_half(src_words, grouped, codes, scales, h, pools):
+            g32 = grouped[:].bitcast(F32).rearrange("p (b r j u) -> p b r j u", r=2, j=P, u=2)
+            for bb in range(2):
+                b = 2 * h + bb
+                xt = pools[bb][0].tile([P, 2, 2, P], F32, name="xt", tag=pools[bb][1])
+                for r in range(2):
+                    for u in range(2):
+                        nc.tensor.transpose(
+                            xt[:, r, u, :], src_words[:, 2 * b + r, P * u : P * u + P], ident_f[:]
+                        )
+                src = xt[:].rearrange("p r u j -> p r j u")
+                if bb == 0:
+                    nc.vector.tensor_copy(out=g32[:, b], in_=src)
+                else:
+                    nc.scalar.copy(out=g32[:, b], in_=src)
+            nc.vector.quantize_mx(
+                out=codes[:, 512 * h : 512 * h + 512].bitcast(FP8X4),
+                scales=scales[:, 512 * h : 512 * h + 512],
+                in_=grouped[:, 2048 * h : 2048 * h + 2048],
+            )
+
+        k_words = k_sb[:].rearrange("p c t d -> p (c t) d").bitcast(F32)
+        q_words = q_sb[:].bitcast(F32)
+        turn_half(k_words, kg, kc, ks, 0, [(psz, "psz"), (psz, "psz")])
+        turn_half(k_words, kg, kc, ks, 1, [(psz, "psz"), (psz, "psz")])
+        turn_half(q_words, qg, qc, qs, 0, [(pst, "pst"), (pso, "pso")])
+        turn_half(q_words, qg, qc, qs, 1, [(pst, "pst"), (pso, "pso")])
+
+        sg = keep.tile([P, 2, D, 4], BF16, name="sg", align_bytes=64)
+        sc = keep.tile([P, 2, D], U32, name="sc", align_bytes=64)
+        ss = keep.tile([P, 2, D], U8, name="ss", align_bytes=64)
+        for c in range(2):
+            nc.vector.tensor_copy(
+                out=sg[:, c].rearrange("p (a i) t -> p a t i", i=4),
+                in_=s_sb[:, c].rearrange("p t (a i) -> p a t i", i=4),
+            )
+        for c in range(2):
+            nc.vector.quantize_mx(
+                out=sc[:, c, :].bitcast(FP8X4),
+                scales=ss[:, c, :],
+                in_=sg[:, c].rearrange("p d t -> p (d t)"),
+            )
+
+        for i in range(NT):
+            zs = []
+            mx2 = small.tile([P, 2], F32, name="mx2", tag="mx2")
+            for n in range(2):
+                z = psz.tile([P, 512], F32, name="z", tag="psz")
+                nc.tensor.matmul_mx(
+                    out=z[:],
+                    lhsT=qc[:, P * i : P * i + P].bitcast(FP8X4),
+                    lhsT_scale=qs[:, P * i : P * i + P],
+                    rhs=kc[:, 512 * n : 512 * n + 512].bitcast(FP8X4),
+                    rhs_scale=ks[:, 512 * n : 512 * n + 512],
+                    start=True,
+                    stop=True,
+                )
+                nc.vector.tensor_reduce(out=mx2[:, n : n + 1], in_=z[:], axis=AX.X, op=ALU.max)
+                zs.append(z)
+            nm = small.tile([P, 1], F32, name="nm", tag="nm")
+            nc.vector.tensor_scalar(
+                out=nm[:], in0=mx2[:, 0:1], scalar1=mx2[:, 1:2], scalar2=-inv_sqrt_d, op0=ALU.max, op1=ALU.mult
+            )
+            e_sb = work.tile([P, T], BF16, name="e_sb", tag="e_sb")
+            sums = small.tile([P, 2], F32, name="sums", tag="sums")
+            for n in range(2):
+                nc.scalar.activation(
+                    out=e_sb[:, 512 * n : 512 * n + 512],
+                    in_=zs[n][:],
+                    func=ACT.Exp,
+                    bias=nm[:, 0:1],
+                    scale=inv_sqrt_d,
+                    accum_out=sums[:, n : n + 1],
+                )
+            et = pst.tile([P, NT, P], BF16, name="et", tag="pst")
+            for kb in range(NT):
+                nc.tensor.transpose(et[:, kb, :], e_sb[:, P * kb : P * kb + P], ident_b[:])
+            eg = work.tile([P, 2, P, 4], BF16, name="eg", tag="eg", align_bytes=64)
+            nc.scalar.copy(out=eg[:], in_=et[:].rearrange("p (c t) j -> p c j t", t=4))
+            ec = work.tile([P, 2 * P], U32, name="ec", tag="ec", align_bytes=64)
+            es = work.tile([P, 2 * P], U8, name="es", tag="es", align_bytes=64)
+            nc.vector.quantize_mx(
+                out=ec[:].bitcast(FP8X4), scales=es[:], in_=eg[:].rearrange("p c j t -> p (c j t)")
+            )
+            o_ps = pso.tile([P, D], F32, name="o_ps", tag="pso")
+            for c in range(2):
+                nc.tensor.matmul_mx(
+                    out=o_ps[:],
+                    lhsT=ec[:, P * c : P * c + P].bitcast(FP8X4),
+                    lhsT_scale=es[:, P * c : P * c + P],
+                    rhs=sc[:, c, :].bitcast(FP8X4),
+                    rhs_scale=ss[:, c, :],
+                    start=(c == 0),
+                    stop=(c == 1),
+                )
+            rs = small.tile([P, 1], F32, name="rs", tag="rs")
+            nc.vector.tensor_tensor(out=rs[:], in0=sums[:, 0:1], in1=sums[:, 1:2], op=ALU.add)
+            rinv = small.tile([P, 1], F32, name="rinv", tag="rinv")
+            nc.vector.reciprocal(out=rinv[:], in_=rs[:])
+            res = work.tile([P, D], F32, name="res", tag="res")
+            nc.vector.scalar_tensor_tensor(
+                out=res[:], in0=o_ps[:], scalar=rinv[:, 0:1], in1=v_sb[:, i, :], op0=ALU.mult, op1=ALU.mult
+            )
+            nc.sync.dma_start(out=o_view[:, i, :], in_=res[:])

@@ -19,52 +19,47 @@ P = 128
 T = 1024
 D = 512
 NT = T // P
+F_LAG = 2
 
 
 def tile_sourceawareattention_kernel(tc, q, k, v, s, out):
     nc = tc.nc
     inv_sqrt_d = 1.0 / math.sqrt(D)
 
-    q2 = q.flatten_outer_dims()
-    k2 = k.flatten_outer_dims()
-    v2 = v.flatten_outer_dims()
-    s2 = s.flatten_outer_dims()
-    o2 = out.flatten_outer_dims()
-
-    q_view = q2.rearrange("(p i) d -> p i d", i=NT)
-    v_view = v2.rearrange("(p i) d -> p i d", i=NT)
-    o_view = o2.rearrange("(p i) d -> p i d", i=NT)
-    k_view = k2.rearrange("(c p t) d -> p c t d", c=2, t=4)
-    s_view = s2.rearrange("(c p t) d -> p c t d", c=2, t=4)
+    q_view = q.flatten_outer_dims().rearrange("(p i) d -> p i d", i=NT)
+    v_view = v.flatten_outer_dims().rearrange("(p i) d -> p i d", i=NT)
+    o_view = out.flatten_outer_dims().rearrange("(p i) d -> p i d", i=NT)
+    k_view = k.flatten_outer_dims().rearrange("(c p t) d -> p c t d", c=2, t=4)
+    s_view = s.flatten_outer_dims().rearrange("(c p t) d -> p c t d", c=2, t=4)
 
     with ExitStack() as ctx:
-        const = ctx.enter_context(tc.tile_pool(name="const", bufs=1))
         keep = ctx.enter_context(tc.tile_pool(name="keep", bufs=1))
-        work = ctx.enter_context(tc.tile_pool(name="work", bufs=3))
-        small = ctx.enter_context(tc.tile_pool(name="small", bufs=4))
-        psz = ctx.enter_context(tc.psum_pool(name="psz", bufs=4))
-        pst = ctx.enter_context(tc.psum_pool(name="pst", bufs=2))
-        pso = ctx.enter_context(tc.psum_pool(name="pso", bufs=2))
+        psum = ctx.enter_context(tc.psum_pool(name="psum", bufs=1))
+        ctx.enter_context(tc.manual_schedule())
+
+        def bank(n, shape, dtype):
+            return psum.tile(shape, dtype, name="bank%d" % n, tag="bank%d" % n)
 
         k_sb = keep.tile([P, 2, 4, D], BF16, name="k_sb")
         q_sb = keep.tile([P, NT, D], BF16, name="q_sb")
         s_sb = keep.tile([P, 2, 4, D], BF16, name="s_sb")
         v_sb = keep.tile([P, NT, D], BF16, name="v_sb")
+        nc.sync.dma_start(out=q_sb[:, 0:2, :], in_=q_view[:, 0:2, :])
         for c in range(2):
             nc.sync.dma_start(out=k_sb[:, c], in_=k_view[:, c])
-        for h in range(2):
-            nc.sync.dma_start(out=q_sb[:, 4 * h : 4 * h + 4, :], in_=q_view[:, 4 * h : 4 * h + 4, :])
+        nc.sync.dma_start(out=q_sb[:, 2:4, :], in_=q_view[:, 2:4, :])
+        nc.sync.dma_start(out=q_sb[:, 4:8, :], in_=q_view[:, 4:8, :])
         for c in range(2):
             nc.sync.dma_start(out=s_sb[:, c], in_=s_view[:, c])
         for h in range(2):
             nc.sync.dma_start(out=v_sb[:, 4 * h : 4 * h + 4, :], in_=v_view[:, 4 * h : 4 * h + 4, :])
 
-        ident_f = const.tile([P, P], F32, name="ident_f")
+        ident_f = keep.tile([P, P], F32, name="ident_f")
         make_identity(nc, ident_f[:])
-        ident_b = const.tile([P, P], BF16, name="ident_b")
+        ident_b = keep.tile([P, P], BF16, name="ident_b")
         make_identity(nc, ident_b[:])
-        warm_in = const.tile([P, 1], F32, name="warm_in")
-        warm_out = const.tile([P, 1], F32, name="warm_out")
+        warm_in = keep.tile([P, 1], F32, name="warm_in")
+        warm_out = keep.tile([P, 1], F32, name="warm_out")
         nc.vector.memset(warm_in[:], 0.0)
         nc.scalar.activation(out=warm_out[:], in_=warm_in[:], func=ACT.Exp)
 
@@ -74,55 +69,54 @@ def tile_sourceawareattention_kernel(tc, q, k, v, s, out):
         qc = keep.tile([P, T], U32, name="qc", align_bytes=64)
         ks = keep.tile([P, T], U8, name="ks", align_bytes=64)
         qs = keep.tile([P, T], U8, name="qs", align_bytes=64)
-
-        def turn_half(src_words, grouped, codes, scales, h, pools):
-            g32 = grouped[:].bitcast(F32).rearrange("p (b r j u) -> p b r j u", r=2, j=P, u=2)
-            for bb in range(2):
-                b = 2 * h + bb
-                xt = pools[bb][0].tile([P, 2, 2, P], F32, name="xt", tag=pools[bb][1])
-                for r in range(2):
-                    for u in range(2):
-                        nc.tensor.transpose(
-                            xt[:, r, u, :], src_words[:, 2 * b + r, P * u : P * u + P], ident_f[:]
-                        )
-                src = xt[:].rearrange("p r u j -> p r j u")
-                if bb == 0:
-                    nc.vector.tensor_copy(out=g32[:, b], in_=src)
-                else:
-                    nc.scalar.copy(out=g32[:, b], in_=src)
-            nc.vector.quantize_mx(
-                out=codes[:, 512 * h : 512 * h + 512].bitcast(FP8X4),
-                scales=scales[:, 512 * h : 512 * h + 512],
-                in_=grouped[:, 2048 * h : 2048 * h + 2048],
-            )
-
-        k_words = k_sb[:].rearrange("p c t d -> p (c t) d").bitcast(F32)
-        q_words = q_sb[:].bitcast(F32)
-        turn_half(k_words, kg, kc, ks, 0, [(psz, "psz"), (psz, "psz")])
-        turn_half(k_words, kg, kc, ks, 1, [(psz, "psz"), (psz, "psz")])
-        turn_half(q_words, qg, qc, qs, 0, [(pst, "pst"), (pso, "pso")])
-        turn_half(q_words, qg, qc, qs, 1, [(pst, "pst"), (pso, "pso")])
-
         sg = keep.tile([P, 2, D, 4], BF16, name="sg", align_bytes=64)
         sc = keep.tile([P, 2, D], U32, name="sc", align_bytes=64)
         ss = keep.tile([P, 2, D], U8, name="ss", align_bytes=64)
-        for c in range(2):
-            nc.vector.tensor_copy(
-                out=sg[:, c].rearrange("p (a i) t -> p a t i", i=4),
-                in_=s_sb[:, c].rearrange("p t (a i) -> p a t i", i=4),
-            )
-        for c in range(2):
+        e_sb = keep.tile([P, NT, T], BF16, name="e_sb")
+        eg = keep.tile([P, NT, 2, P, 4], BF16, name="eg", align_bytes=64)
+        ec = keep.tile([P, NT, 2 * P], U32, name="ec", align_bytes=64)
+        es = keep.tile([P, NT, 2 * P], U8, name="es", align_bytes=64)
+        res = keep.tile([P, NT, D], F32, name="res")
+        mx2 = keep.tile([P, NT, 2], F32, name="mx2")
+        nm = keep.tile([P, NT], F32, name="nm")
+        sums = keep.tile([P, NT, 2], F32, name="sums")
+        rs = keep.tile([P, NT], F32, name="rs")
+        rinv = keep.tile([P, NT], F32, name="rinv")
+
+        words = {
+            "k": k_sb[:].rearrange("p c t d -> p (c t) d").bitcast(F32),
+            "q": q_sb[:].bitcast(F32),
+        }
+        grouped = {"k": kg, "q": qg}
+        codes = {"k": kc, "q": qc}
+        scales = {"k": ks, "q": qs}
+        live = {}
+
+        def turn(x, b, n):
+            xt = bank(n, [P, 2, 2, P], F32)
+            for r in range(2):
+                for u in range(2):
+                    nc.tensor.transpose(xt[:, r, u, :], words[x][:, 2 * b + r, P * u : P * u + P], ident_f[:])
+            live[(x, b)] = xt
+
+        def evac(x, b, on_vector):
+            g32 = grouped[x][:].bitcast(F32).rearrange("p (b r j u) -> p b r j u", r=2, j=P, u=2)
+            src = live[(x, b)][:].rearrange("p r u j -> p r j u")
+            if on_vector:
+                nc.vector.tensor_copy(out=g32[:, b], in_=src)
+            else:
+                nc.scalar.copy(out=g32[:, b], in_=src)
+
+        def quant(x, first, cols):
             nc.vector.quantize_mx(
-                out=sc[:, c, :].bitcast(FP8X4),
-                scales=ss[:, c, :],
-                in_=sg[:, c].rearrange("p d t -> p (d t)"),
+                out=codes[x][:, first : first + cols].bitcast(FP8X4),
+                scales=scales[x][:, first : first + cols],
+                in_=grouped[x][:, 4 * first : 4 * (first + cols)],
             )
 
-        for i in range(NT):
-            zs = []
-            mx2 = small.tile([P, 2], F32, name="mx2", tag="mx2")
+        def scores(i):
             for n in range(2):
-                z = psz.tile([P, 512], F32, name="z", tag="psz")
+                z = bank((2 * i + n) % 6, [P, 512], F32)
                 nc.tensor.matmul_mx(
                     out=z[:],
                     lhsT=qc[:, P * i : P * i + P].bitcast(FP8X4),
@@ -132,50 +126,132 @@ def tile_sourceawareattention_kernel(tc, q, k, v, s, out):
                     start=True,
                     stop=True,
                 )
-                nc.vector.tensor_reduce(out=mx2[:, n : n + 1], in_=z[:], axis=AX.X, op=ALU.max)
-                zs.append(z)
-            nm = small.tile([P, 1], F32, name="nm", tag="nm")
+                live[("z", i, n)] = z
+
+        def row_max(i):
+            for n in range(2):
+                nc.vector.tensor_reduce(out=mx2[:, i, n : n + 1], in_=live[("z", i, n)][:], axis=AX.X, op=ALU.max)
             nc.vector.tensor_scalar(
-                out=nm[:], in0=mx2[:, 0:1], scalar1=mx2[:, 1:2], scalar2=-inv_sqrt_d, op0=ALU.max, op1=ALU.mult
+                out=nm[:, i : i + 1],
+                in0=mx2[:, i, 0:1],
+                scalar1=mx2[:, i, 1:2],
+                scalar2=-inv_sqrt_d,
+                op0=ALU.max,
+                op1=ALU.mult,
             )
-            e_sb = work.tile([P, T], BF16, name="e_sb", tag="e_sb")
-            sums = small.tile([P, 2], F32, name="sums", tag="sums")
+
+        def exps(i):
             for n in range(2):
                 nc.scalar.activation(
-                    out=e_sb[:, 512 * n : 512 * n + 512],
-                    in_=zs[n][:],
+                    out=e_sb[:, i, 512 * n : 512 * n + 512],
+                    in_=live[("z", i, n)][:],
                     func=ACT.Exp,
-                    bias=nm[:, 0:1],
+                    bias=nm[:, i : i + 1],
                     scale=inv_sqrt_d,
-                    accum_out=sums[:, n : n + 1],
+                    accum_out=sums[:, i, n : n + 1],
                 )
-            et = pst.tile([P, NT, P], BF16, name="et", tag="pst")
+
+        def turn_e(i):
+            et = bank((6, 7, 4, 5)[i % 4], [P, NT, P], BF16)
             for kb in range(NT):
-                nc.tensor.transpose(et[:, kb, :], e_sb[:, P * kb : P * kb + P], ident_b[:])
-            eg = work.tile([P, 2, P, 4], BF16, name="eg", tag="eg", align_bytes=64)
-            nc.scalar.copy(out=eg[:], in_=et[:].rearrange("p (c t) j -> p c j t", t=4))
-            ec = work.tile([P, 2 * P], U32, name="ec", tag="ec", align_bytes=64)
-            es = work.tile([P, 2 * P], U8, name="es", tag="es", align_bytes=64)
+                nc.tensor.transpose(et[:, kb, :], e_sb[:, i, P * kb : P * kb + P], ident_b[:])
+            live[("et", i)] = et
+
+        def evac_e(i):
+            nc.scalar.copy(out=eg[:, i], in_=live[("et", i)][:].rearrange("p (c t) j -> p c j t", t=4))
+
+        def quant_e(i):
             nc.vector.quantize_mx(
-                out=ec[:].bitcast(FP8X4), scales=es[:], in_=eg[:].rearrange("p c j t -> p (c j t)")
+                out=ec[:, i, :].bitcast(FP8X4),
+                scales=es[:, i, :],
+                in_=eg[:, i].rearrange("p c j t -> p (c j t)"),
             )
-            o_ps = pso.tile([P, D], F32, name="o_ps", tag="pso")
+
+        def weigh(i):
+            o_ps = bank(i % 4, [P, D], F32)
             for c in range(2):
                 nc.tensor.matmul_mx(
                     out=o_ps[:],
-                    lhsT=ec[:, P * c : P * c + P].bitcast(FP8X4),
-                    lhsT_scale=es[:, P * c : P * c + P],
+                    lhsT=ec[:, i, P * c : P * c + P].bitcast(FP8X4),
+                    lhsT_scale=es[:, i, P * c : P * c + P],
                     rhs=sc[:, c, :].bitcast(FP8X4),
                     rhs_scale=ss[:, c, :],
                     start=(c == 0),
                     stop=(c == 1),
                 )
-            rs = small.tile([P, 1], F32, name="rs", tag="rs")
-            nc.vector.tensor_tensor(out=rs[:], in0=sums[:, 0:1], in1=sums[:, 1:2], op=ALU.add)
-            rinv = small.tile([P, 1], F32, name="rinv", tag="rinv")
-            nc.vector.reciprocal(out=rinv[:], in_=rs[:])
-            res = work.tile([P, D], F32, name="res", tag="res")
+            live[("o", i)] = o_ps
+
+        def finish(i):
             nc.vector.scalar_tensor_tensor(
-                out=res[:], in0=o_ps[:], scalar=rinv[:, 0:1], in1=v_sb[:, i, :], op0=ALU.mult, op1=ALU.mult
+                out=res[:, i, :],
+                in0=live[("o", i)][:],
+                scalar=rinv[:, i : i + 1],
+                in1=v_sb[:, i, :],
+                op0=ALU.mult,
+                op1=ALU.mult,
             )
-            nc.sync.dma_start(out=o_view[:, i, :], in_=res[:])
+            nc.sync.dma_start(out=o_view[:, i, :], in_=res[:, i, :])
+
+        turn("q", 0, 6)
+        evac("q", 0, True)
+        quant("q", 0, 256)
+        turn("k", 0, 0)
+        turn("k", 1, 1)
+        evac("k", 0, True)
+        evac("k", 1, False)
+        quant("k", 0, 512)
+        turn("k", 2, 2)
+        turn("k", 3, 3)
+        evac("k", 2, True)
+        evac("k", 3, False)
+        quant("k", 512, 512)
+        turn("q", 1, 7)
+        evac("q", 1, False)
+        scores(0)
+        scores(1)
+        row_max(0)
+        quant("q", 256, 256)
+        scores(2)
+        row_max(1)
+        row_max(2)
+
+        for i in range(NT):
+            exps(i)
+            if i == 0:
+                turn("q", 2, 6)
+                turn("q", 3, 7)
+                evac("q", 2, False)
+                evac("q", 3, False)
+                quant("q", 512, 256)
+                quant("q", 768, 256)
+            if i + 3 < NT:
+                scores(i + 3)
+                row_max(i + 3)
+            if i == 1:
+                turn_e(0)
+                turn_e(1)
+            if i == 5:
+                turn_e(2)
+                turn_e(3)
+
+        for c in range(2):
+            nc.vector.tensor_copy(
+                out=sg[:, c].rearrange("p (a i) t -> p a t i", i=4),
+                in_=s_sb[:, c].rearrange("p t (a i) -> p a t i", i=4),
+            )
+        for c in range(2):
+            nc.vector.quantize_mx(
+                out=sc[:, c, :].bitcast(FP8X4), scales=ss[:, c, :], in_=sg[:, c].rearrange("p d t -> p (d t)")
+            )
+        nc.vector.tensor_reduce(out=rs[:], in_=sums[:], axis=AX.X, op=ALU.add)
+        nc.vector.reciprocal(out=rinv[:], in_=rs[:])
+
+        for i in range(NT + F_LAG):
+            if i < NT:
+                evac_e(i)
+                if i + 4 < NT:
+                    turn_e(i + 4)
+                quant_e(i)
+                weigh(i)
+            if i >= F_LAG:
+                finish(i - F_LAG)

@@ -20,6 +20,7 @@ T = 1024
 D = 512
 NT = T // P
 F_LAG = 2
+E_BANKS = (6, 7, 4, 5, 0, 1, 2, 3)
 
 
 def tile_sourceawareattention_kernel(tc, q, k, v, s, out):
@@ -46,9 +47,10 @@ def tile_sourceawareattention_kernel(tc, q, k, v, s, out):
         v_sb = keep.tile([P, NT, D], BF16, name="v_sb")
         nc.sync.dma_start(out=q_sb[:, 0:2, :], in_=q_view[:, 0:2, :])
         for c in range(2):
-            nc.sync.dma_start(out=k_sb[:, c], in_=k_view[:, c])
-        nc.sync.dma_start(out=q_sb[:, 2:4, :], in_=q_view[:, 2:4, :])
-        nc.sync.dma_start(out=q_sb[:, 4:8, :], in_=q_view[:, 4:8, :])
+            for h in range(2):
+                nc.sync.dma_start(out=k_sb[:, c, 2 * h : 2 * h + 2, :], in_=k_view[:, c, 2 * h : 2 * h + 2, :])
+        for b in range(1, 4):
+            nc.sync.dma_start(out=q_sb[:, 2 * b : 2 * b + 2, :], in_=q_view[:, 2 * b : 2 * b + 2, :])
         for c in range(2):
             nc.sync.dma_start(out=s_sb[:, c], in_=s_view[:, c])
         for h in range(2):
@@ -152,7 +154,7 @@ def tile_sourceawareattention_kernel(tc, q, k, v, s, out):
                 )
 
         def turn_e(i):
-            et = bank((6, 7, 4, 5)[i % 4], [P, NT, P], BF16)
+            et = bank(E_BANKS[i], [P, NT, P], BF16)
             for kb in range(NT):
                 nc.tensor.transpose(et[:, kb, :], e_sb[:, i, P * kb : P * kb + P], ident_b[:])
             live[("et", i)] = et
@@ -168,7 +170,7 @@ def tile_sourceawareattention_kernel(tc, q, k, v, s, out):
             )
 
         def weigh(i):
-            o_ps = bank(i % 4, [P, D], F32)
+            o_ps = bank(E_BANKS[i], [P, D], F32)
             for c in range(2):
                 nc.tensor.matmul_mx(
                     out=o_ps[:],
@@ -195,44 +197,39 @@ def tile_sourceawareattention_kernel(tc, q, k, v, s, out):
         turn("q", 0, 6)
         evac("q", 0, True)
         quant("q", 0, 256)
-        turn("k", 0, 0)
-        turn("k", 1, 1)
-        evac("k", 0, True)
-        evac("k", 1, False)
-        quant("k", 0, 512)
-        turn("k", 2, 2)
-        turn("k", 3, 3)
-        evac("k", 2, True)
-        evac("k", 3, False)
-        quant("k", 512, 512)
+        for b in range(4):
+            turn("k", b, b)
+            evac("k", b, b % 2 == 0)
+            if b >= 1:
+                quant("k", 256 * (b - 1), 256)
+        quant("k", 768, 256)
         turn("q", 1, 7)
         evac("q", 1, False)
-        scores(0)
-        scores(1)
-        row_max(0)
         quant("q", 256, 256)
+        turn("q", 2, 6)
+        evac("q", 2, False)
+        scores(0)
+        turn("q", 3, 7)
+        evac("q", 3, False)
+        scores(1)
         scores(2)
+        row_max(0)
+        quant("q", 512, 256)
         row_max(1)
         row_max(2)
+        quant("q", 768, 256)
 
         for i in range(NT):
             exps(i)
-            if i == 0:
-                turn("q", 2, 6)
-                turn("q", 3, 7)
-                evac("q", 2, False)
-                evac("q", 3, False)
-                quant("q", 512, 256)
-                quant("q", 768, 256)
             if i + 3 < NT:
                 scores(i + 3)
                 row_max(i + 3)
             if i == 1:
                 turn_e(0)
                 turn_e(1)
-            if i == 5:
-                turn_e(2)
-                turn_e(3)
+            if i >= 5:
+                turn_e(2 * i - 8)
+                turn_e(2 * i - 7)
 
         for c in range(2):
             nc.vector.tensor_copy(
@@ -249,8 +246,6 @@ def tile_sourceawareattention_kernel(tc, q, k, v, s, out):
         for i in range(NT + F_LAG):
             if i < NT:
                 evac_e(i)
-                if i + 4 < NT:
-                    turn_e(i + 4)
                 quant_e(i)
                 weigh(i)
             if i >= F_LAG:

@@ -51,10 +51,10 @@ def tile_sourceawareattention_kernel(tc, q, k, v, s, out):
                 nc.sync.dma_start(out=k_sb[:, c, 2 * h : 2 * h + 2, :], in_=k_view[:, c, 2 * h : 2 * h + 2, :])
         for b in range(1, 4):
             nc.sync.dma_start(out=q_sb[:, 2 * b : 2 * b + 2, :], in_=q_view[:, 2 * b : 2 * b + 2, :])
-        for c in range(2):
-            nc.sync.dma_start(out=s_sb[:, c], in_=s_view[:, c])
         for h in range(2):
             nc.sync.dma_start(out=v_sb[:, 4 * h : 4 * h + 4, :], in_=v_view[:, 4 * h : 4 * h + 4, :])
+        for c in range(2):
+            nc.sync.dma_start(out=s_sb[:, c], in_=s_view[:, c])
 
         ident_f = keep.tile([P, P], F32, name="ident_f")
         make_identity(nc, ident_f[:])
@@ -159,8 +159,12 @@ def tile_sourceawareattention_kernel(tc, q, k, v, s, out):
                 nc.tensor.transpose(et[:, kb, :], e_sb[:, i, P * kb : P * kb + P], ident_b[:])
             live[("et", i)] = et
 
-        def evac_e(i):
-            nc.scalar.copy(out=eg[:, i], in_=live[("et", i)][:].rearrange("p (c t) j -> p c j t", t=4))
+        def evac_e(i, on_vector):
+            src = live[("et", i)][:].rearrange("p (c t) j -> p c j t", t=4)
+            if on_vector:
+                nc.vector.tensor_copy(out=eg[:, i], in_=src)
+            else:
+                nc.scalar.copy(out=eg[:, i], in_=src)
 
         def quant_e(i):
             nc.vector.quantize_mx(
@@ -194,6 +198,17 @@ def tile_sourceawareattention_kernel(tc, q, k, v, s, out):
             )
             nc.sync.dma_start(out=o_view[:, i, :], in_=res[:, i, :])
 
+        for c in range(2):
+            for h in range(2):
+                nc.gpsimd.tensor_scalar(
+                    out=sg[:, c, 256 * h : 256 * h + 256, :],
+                    in0=s_sb[:, c, :, 256 * h : 256 * h + 256].rearrange("p t d -> p d t"),
+                    scalar1=1.0,
+                    scalar2=0.0,
+                    op0=ALU.mult,
+                    op1=ALU.add,
+                )
+
         turn("q", 0, 6)
         evac("q", 0, True)
         quant("q", 0, 256)
@@ -216,8 +231,8 @@ def tile_sourceawareattention_kernel(tc, q, k, v, s, out):
         row_max(0)
         quant("q", 512, 256)
         row_max(1)
-        row_max(2)
         quant("q", 768, 256)
+        row_max(2)
 
         for i in range(NT):
             exps(i)
@@ -231,11 +246,7 @@ def tile_sourceawareattention_kernel(tc, q, k, v, s, out):
                 turn_e(2 * i - 8)
                 turn_e(2 * i - 7)
 
-        for c in range(2):
-            nc.vector.tensor_copy(
-                out=sg[:, c].rearrange("p (a i) t -> p a t i", i=4),
-                in_=s_sb[:, c].rearrange("p t (a i) -> p a t i", i=4),
-            )
+        evac_e(0, True)
         for c in range(2):
             nc.vector.quantize_mx(
                 out=sc[:, c, :].bitcast(FP8X4), scales=ss[:, c, :], in_=sg[:, c].rearrange("p d t -> p (d t)")
@@ -245,7 +256,8 @@ def tile_sourceawareattention_kernel(tc, q, k, v, s, out):
 
         for i in range(NT + F_LAG):
             if i < NT:
-                evac_e(i)
+                if i > 0:
+                    evac_e(i, False)
                 quant_e(i)
                 weigh(i)
             if i >= F_LAG:

@@ -21,6 +21,7 @@ D = 512
 NT = T // P
 F_LAG = 2
 E_BANKS = (6, 7, 4, 5, 0, 1, 2, 3)
+VECTOR_TILES = (0, 2)
 
 
 def tile_sourceawareattention_kernel(tc, q, k, v, s, out):
@@ -257,7 +258,7 @@ def tile_sourceawareattention_kernel(tc, q, k, v, s, out):
         for i in range(NT + F_LAG):
             if i < NT:
                 if i > 0:
-                    evac_e(i, False)
+                    evac_e(i, i in VECTOR_TILES)
                 quant_e(i)
                 weigh(i)
             if i >= F_LAG:

@@ -20,7 +20,6 @@ T = 1024
 D = 512
 NT = T // P
 F_LAG = 2
-E_BANKS = (6, 7, 4, 5, 0, 1, 2, 3)
 VECTOR_TILES = (0, 2)
 
 
@@ -119,7 +118,7 @@ def tile_sourceawareattention_kernel(tc, q, k, v, s, out):
 
         def scores(i):
             for n in range(2):
-                z = bank((2 * i + n) % 6, [P, 512], F32)
+                z = bank((2 * i + n) % 8, [P, 512], F32)
                 nc.tensor.matmul_mx(
                     out=z[:],
                     lhsT=qc[:, P * i : P * i + P].bitcast(FP8X4),
@@ -155,7 +154,7 @@ def tile_sourceawareattention_kernel(tc, q, k, v, s, out):
                 )
 
         def turn_e(i):
-            et = bank(E_BANKS[i], [P, NT, P], BF16)
+            et = bank(i, [P, NT, P], BF16)
             for kb in range(NT):
                 nc.tensor.transpose(et[:, kb, :], e_sb[:, i, P * kb : P * kb + P], ident_b[:])
             live[("et", i)] = et
@@ -175,7 +174,7 @@ def tile_sourceawareattention_kernel(tc, q, k, v, s, out):
             )
 
         def weigh(i):
-            o_ps = bank(E_BANKS[i], [P, D], F32)
+            o_ps = bank(i, [P, D], F32)
             for c in range(2):
                 nc.tensor.matmul_mx(
                     out=o_ps[:],
@@ -210,7 +209,7 @@ def tile_sourceawareattention_kernel(tc, q, k, v, s, out):
                     op1=ALU.add,
                 )
 
-        turn("q", 0, 6)
+        turn("q", 0, 4)
         evac("q", 0, True)
         quant("q", 0, 256)
         for b in range(4):
@@ -219,7 +218,7 @@ def tile_sourceawareattention_kernel(tc, q, k, v, s, out):
             if b >= 1:
                 quant("k", 256 * (b - 1), 256)
         quant("k", 768, 256)
-        turn("q", 1, 7)
+        turn("q", 1, 5)
         evac("q", 1, False)
         quant("q", 256, 256)
         turn("q", 2, 6)
@@ -229,21 +228,20 @@ def tile_sourceawareattention_kernel(tc, q, k, v, s, out):
         evac("q", 3, False)
         scores(1)
         scores(2)
+        scores(3)
         row_max(0)
         quant("q", 512, 256)
         row_max(1)
         quant("q", 768, 256)
         row_max(2)
+        row_max(3)
 
         for i in range(NT):
             exps(i)
-            if i + 3 < NT:
-                scores(i + 3)
-                row_max(i + 3)
-            if i == 1:
-                turn_e(0)
-                turn_e(1)
-            if i >= 5:
+            if i + 4 < NT:
+                scores(i + 4)
+                row_max(i + 4)
+            else:
                 turn_e(2 * i - 8)
                 turn_e(2 * i - 7)
 

@@ -20,7 +20,6 @@ T = 1024
 D = 512
 NT = T // P
 F_LAG = 2
-VECTOR_TILES = (0, 2)
 
 
 def tile_sourceawareattention_kernel(tc, q, k, v, s, out):
@@ -51,15 +50,13 @@ def tile_sourceawareattention_kernel(tc, q, k, v, s, out):
                 nc.sync.dma_start(out=k_sb[:, c, 2 * h : 2 * h + 2, :], in_=k_view[:, c, 2 * h : 2 * h + 2, :])
         for b in range(1, 4):
             nc.sync.dma_start(out=q_sb[:, 2 * b : 2 * b + 2, :], in_=q_view[:, 2 * b : 2 * b + 2, :])
-        for h in range(2):
-            nc.sync.dma_start(out=v_sb[:, 4 * h : 4 * h + 4, :], in_=v_view[:, 4 * h : 4 * h + 4, :])
         for c in range(2):
             nc.sync.dma_start(out=s_sb[:, c], in_=s_view[:, c])
+        for h in range(2):
+            nc.sync.dma_start(out=v_sb[:, 4 * h : 4 * h + 4, :], in_=v_view[:, 4 * h : 4 * h + 4, :])
 
         ident_f = keep.tile([P, P], F32, name="ident_f")
         make_identity(nc, ident_f[:])
-        ident_b = keep.tile([P, P], BF16, name="ident_b")
-        make_identity(nc, ident_b[:])
         warm_in = keep.tile([P, 1], F32, name="warm_in")
         warm_out = keep.tile([P, 1], F32, name="warm_out")
         nc.vector.memset(warm_in[:], 0.0)
@@ -92,6 +89,7 @@ def tile_sourceawareattention_kernel(tc, q, k, v, s, out):
         grouped = {"k": kg, "q": qg}
         codes = {"k": kc, "q": qc}
         scales = {"k": ks, "q": qs}
+        eg32 = eg[:].rearrange("p i c j t -> p i c (j t)").bitcast(F32).rearrange("p i c (j h) -> p i c j h", h=2)
         live = {}
 
         def turn(x, b, n):
@@ -102,8 +100,12 @@ def tile_sourceawareattention_kernel(tc, q, k, v, s, out):
             live[(x, b)] = xt
 
         def evac(x, b, on_vector):
-            g32 = grouped[x][:].bitcast(F32).rearrange("p (b r j u) -> p b r j u", r=2, j=P, u=2)
-            src = live[(x, b)][:].rearrange("p r u j -> p r j u")
+            if x == "k":
+                g32 = grouped[x][:].bitcast(F32).rearrange("p (b j r u) -> p b j r u", j=P, r=2, u=2)
+                src = live[(x, b)][:].rearrange("p r u j -> p j r u")
+            else:
+                g32 = grouped[x][:].bitcast(F32).rearrange("p (b r j u) -> p b r j u", r=2, j=P, u=2)
+                src = live[(x, b)][:].rearrange("p r u j -> p r j u")
             if on_vector:
                 nc.vector.tensor_copy(out=g32[:, b], in_=src)
             else:
@@ -130,9 +132,10 @@ def tile_sourceawareattention_kernel(tc, q, k, v, s, out):
                 )
                 live[("z", i, n)] = z
 
-        def row_max(i):
-            for n in range(2):
-                nc.vector.tensor_reduce(out=mx2[:, i, n : n + 1], in_=live[("z", i, n)][:], axis=AX.X, op=ALU.max)
+        def half_max(i, n):
+            nc.vector.tensor_reduce(out=mx2[:, i, n : n + 1], in_=live[("z", i, n)][:], axis=AX.X, op=ALU.max)
+
+        def neg_max(i):
             nc.vector.tensor_scalar(
                 out=nm[:, i : i + 1],
                 in0=mx2[:, i, 0:1],
@@ -154,17 +157,18 @@ def tile_sourceawareattention_kernel(tc, q, k, v, s, out):
                 )
 
         def turn_e(i):
-            et = bank(i, [P, NT, P], BF16)
-            for kb in range(NT):
-                nc.tensor.transpose(et[:, kb, :], e_sb[:, i, P * kb : P * kb + P], ident_b[:])
+            et = bank(i, [P, 2, 2, P], F32)
+            e_words = e_sb[:].bitcast(F32)
+            for c in range(2):
+                for h in range(2):
+                    w = 256 * c + P * h
+                    nc.tensor.transpose(et[:, c, h, :], e_words[:, i, w : w + P], ident_f[:])
             live[("et", i)] = et
 
-        def evac_e(i, on_vector):
-            src = live[("et", i)][:].rearrange("p (c t) j -> p c j t", t=4)
-            if on_vector:
-                nc.vector.tensor_copy(out=eg[:, i], in_=src)
-            else:
-                nc.scalar.copy(out=eg[:, i], in_=src)
+        def evac_e(i):
+            src = live[("et", i)][:].rearrange("p c h j -> p c j h")
+            dst = eg32[:, i]
+            nc.scalar.copy(out=dst, in_=src)
 
         def quant_e(i):
             nc.vector.quantize_mx(
@@ -198,7 +202,7 @@ def tile_sourceawareattention_kernel(tc, q, k, v, s, out):
             )
             nc.sync.dma_start(out=o_view[:, i, :], in_=res[:, i, :])
 
-        for c in range(2):
+        def group_s(c):
             for h in range(2):
                 nc.gpsimd.tensor_scalar(
                     out=sg[:, c, 256 * h : 256 * h + 256, :],
@@ -209,55 +213,81 @@ def tile_sourceawareattention_kernel(tc, q, k, v, s, out):
                     op1=ALU.add,
                 )
 
+        def quant_s(c):
+            nc.vector.quantize_mx(
+                out=sc[:, c, :].bitcast(FP8X4), scales=ss[:, c, :], in_=sg[:, c].rearrange("p d t -> p (d t)")
+            )
+
+        def reciprocals(i, n):
+            nc.vector.tensor_reduce(out=rs[:, i : i + n], in_=sums[:, i : i + n, :], axis=AX.X, op=ALU.add)
+            nc.vector.reciprocal(out=rinv[:, i : i + n], in_=rs[:, i : i + n])
+
         turn("q", 0, 4)
         evac("q", 0, True)
-        quant("q", 0, 256)
         for b in range(4):
-            turn("k", b, b)
-            evac("k", b, b % 2 == 0)
+            turn("k", b, (5, 6, 7, 4)[b])
+            evac("k", b, b == 1)
+            if b == 1:
+                quant("q", 0, 256)
             if b >= 1:
                 quant("k", 256 * (b - 1), 256)
         quant("k", 768, 256)
         turn("q", 1, 5)
         evac("q", 1, False)
-        quant("q", 256, 256)
-        turn("q", 2, 6)
-        evac("q", 2, False)
         scores(0)
-        turn("q", 3, 7)
-        evac("q", 3, False)
         scores(1)
+        turn("q", 2, 6)
+        turn("q", 3, 7)
+        half_max(0, 0)
+        half_max(0, 1)
+        quant("q", 256, 256)
+        neg_max(0)
         scores(2)
+        exps(0)
+        evac("q", 2, False)
+        evac("q", 3, False)
         scores(3)
-        row_max(0)
+        half_max(1, 0)
+        half_max(1, 1)
+        half_max(2, 0)
+        neg_max(1)
+        half_max(2, 1)
         quant("q", 512, 256)
-        row_max(1)
+        neg_max(2)
         quant("q", 768, 256)
-        row_max(2)
-        row_max(3)
-
-        for i in range(NT):
-            exps(i)
-            if i + 4 < NT:
-                scores(i + 4)
-                row_max(i + 4)
-            else:
-                turn_e(2 * i - 8)
-                turn_e(2 * i - 7)
-
-        evac_e(0, True)
+        half_max(3, 0)
+        half_max(3, 1)
         for c in range(2):
-            nc.vector.quantize_mx(
-                out=sc[:, c, :].bitcast(FP8X4), scales=ss[:, c, :], in_=sg[:, c].rearrange("p d t -> p (d t)")
-            )
-        nc.vector.tensor_reduce(out=rs[:], in_=sums[:], axis=AX.X, op=ALU.add)
-        nc.vector.reciprocal(out=rinv[:], in_=rs[:])
+            group_s(c)
 
-        for i in range(NT + F_LAG):
-            if i < NT:
-                if i > 0:
-                    evac_e(i, i in VECTOR_TILES)
-                quant_e(i)
-                weigh(i)
-            if i >= F_LAG:
-                finish(i - F_LAG)
+        for i in range(NT // 2):
+            if i > 0:
+                exps(i)
+            scores(i + 4)
+            half_max(i + 4, 0)
+            neg_max(i + 3)
+            half_max(i + 4, 1)
+
+        for p in range(NT // 2 + 1):
+            if p < NT // 2:
+                exps(4 + p)
+                turn_e(2 * p)
+                turn_e(2 * p + 1)
+            if p == 0:
+                quant_s(0)
+                neg_max(7)
+            else:
+                for i in (2 * p - 2, 2 * p - 1):
+                    evac_e(i)
+                for i in (2 * p - 2, 2 * p - 1):
+                    if i >= F_LAG:
+                        finish(i - F_LAG)
+                    quant_e(i)
+                    if i == 0:
+                        quant_s(1)
+                    if i % 4 == 1:
+                        reciprocals(i - 1, 4)
+                for i in (2 * p - 2, 2 * p - 1):
+                    weigh(i)
+        finish(6)
+        finish(7)

@@ -68,7 +68,6 @@ def tile_sourceawareattention_kernel(tc, q, k, v, s, out):
         qc = keep.tile([P, T], U32, name="qc", align_bytes=64)
         ks = keep.tile([P, T], U8, name="ks", align_bytes=64)
         qs = keep.tile([P, T], U8, name="qs", align_bytes=64)
-        sg = keep.tile([P, 2, D, 4], BF16, name="sg", align_bytes=64)
         sc = keep.tile([P, 2, D], U32, name="sc", align_bytes=64)
         ss = keep.tile([P, 2, D], U8, name="ss", align_bytes=64)
         e_sb = keep.tile([P, NT, T], BF16, name="e_sb")
@@ -91,6 +90,7 @@ def tile_sourceawareattention_kernel(tc, q, k, v, s, out):
         scales = {"k": ks, "q": qs}
         eg32 = eg[:].rearrange("p i c j t -> p i c (j t)").bitcast(F32).rearrange("p i c (j h) -> p i c j h", h=2)
         live = {}
+        sg = [qg[:, 2048 * (1 - c) : 2048 * (1 - c) + 2048].rearrange("p (d t) -> p d t", t=4) for c in range(2)]
 
         def turn(x, b, n):
             xt = bank(n, [P, 2, 2, P], F32)
@@ -203,9 +203,9 @@ def tile_sourceawareattention_kernel(tc, q, k, v, s, out):
             nc.sync.dma_start(out=o_view[:, i, :], in_=res[:, i, :])
 
         def group_s(c):
-            for h in range(2):
+            for h in (1, 0):
                 nc.gpsimd.tensor_scalar(
-                    out=sg[:, c, 256 * h : 256 * h + 256, :],
+                    out=sg[c][:, 256 * h : 256 * h + 256, :],
                     in0=s_sb[:, c, :, 256 * h : 256 * h + 256].rearrange("p t d -> p d t"),
                     scalar1=1.0,
                     scalar2=0.0,
@@ -215,7 +215,7 @@ def tile_sourceawareattention_kernel(tc, q, k, v, s, out):
 
         def quant_s(c):
             nc.vector.quantize_mx(
-                out=sc[:, c, :].bitcast(FP8X4), scales=ss[:, c, :], in_=sg[:, c].rearrange("p d t -> p (d t)")
+                out=sc[:, c, :].bitcast(FP8X4), scales=ss[:, c, :], in_=sg[c].rearrange("p d t -> p (d t)")
             )
 
         def reciprocals(i, n):

@@ -19,7 +19,7 @@ P = 128
 T = 1024
 D = 512
 NT = T // P
-F_LAG = 2
+F_LAG = 3
 
 
 def tile_sourceawareattention_kernel(tc, q, k, v, s, out):
@@ -218,8 +218,10 @@ def tile_sourceawareattention_kernel(tc, q, k, v, s, out):
                 out=sc[:, c, :].bitcast(FP8X4), scales=ss[:, c, :], in_=sg[c].rearrange("p d t -> p (d t)")
             )
 
-        def reciprocals(i, n):
+        def row_sums(i, n):
             nc.vector.tensor_reduce(out=rs[:, i : i + n], in_=sums[:, i : i + n, :], axis=AX.X, op=ALU.add)
+
+        def reciprocals(i, n):
             nc.vector.reciprocal(out=rinv[:, i : i + n], in_=rs[:, i : i + n])
 
         turn("q", 0, 4)
@@ -276,6 +278,7 @@ def tile_sourceawareattention_kernel(tc, q, k, v, s, out):
             if p == 0:
                 quant_s(0)
                 neg_max(7)
+                row_sums(0, 4)
             else:
                 for i in (2 * p - 2, 2 * p - 1):
                     evac_e(i)
@@ -285,9 +288,12 @@ def tile_sourceawareattention_kernel(tc, q, k, v, s, out):
                     quant_e(i)
                     if i == 0:
                         quant_s(1)
-                    if i % 4 == 1:
-                        reciprocals(i - 1, 4)
+                        reciprocals(0, 4)
+                    if i == 5:
+                        row_sums(4, 4)
+                    if i == 6:
+                        reciprocals(4, 4)
                 for i in (2 * p - 2, 2 * p - 1):
                     weigh(i)
-        finish(6)
-        finish(7)
+        for i in range(NT - F_LAG, NT):
+            finish(i)

@@ -44,12 +44,12 @@ def tile_sourceawareattention_kernel(tc, q, k, v, s, out):
         q_sb = keep.tile([P, NT, D], BF16, name="q_sb")
         s_sb = keep.tile([P, 2, 4, D], BF16, name="s_sb")
         v_sb = keep.tile([P, NT, D], BF16, name="v_sb")
-        nc.sync.dma_start(out=q_sb[:, 0:2, :], in_=q_view[:, 0:2, :])
+        nc.sync.dma_start(out=q_sb[:, 0:1, :], in_=q_view[:, 0:1, :])
         for c in range(2):
             for h in range(2):
                 nc.sync.dma_start(out=k_sb[:, c, 2 * h : 2 * h + 2, :], in_=k_view[:, c, 2 * h : 2 * h + 2, :])
-        for b in range(1, 4):
-            nc.sync.dma_start(out=q_sb[:, 2 * b : 2 * b + 2, :], in_=q_view[:, 2 * b : 2 * b + 2, :])
+        for i, j in ((1, 4), (4, 8)):
+            nc.sync.dma_start(out=q_sb[:, i:j, :], in_=q_view[:, i:j, :])
         for c in range(2):
             nc.sync.dma_start(out=s_sb[:, c], in_=s_view[:, c])
         for h in range(2):
@@ -92,26 +92,28 @@ def tile_sourceawareattention_kernel(tc, q, k, v, s, out):
         live = {}
         sg = [qg[:, 2048 * (1 - c) : 2048 * (1 - c) + 2048].rearrange("p (d t) -> p d t", t=4) for c in range(2)]
 
-        def turn(x, b, n):
-            xt = bank(n, [P, 2, 2, P], F32)
-            for r in range(2):
+        def turn(x, first, count, n):
+            xt = bank(n, [P, count, 2, P], F32)
+            for r in range(count):
                 for u in range(2):
-                    nc.tensor.transpose(xt[:, r, u, :], words[x][:, 2 * b + r, P * u : P * u + P], ident_f[:])
-            live[(x, b)] = xt
+                    nc.tensor.transpose(xt[:, r, u, :], words[x][:, first + r, P * u : P * u + P], ident_f[:])
+            live[(x, first)] = xt
 
-        def evac(x, b, on_vector):
+        def evac(x, first, count, on_vector):
+            g32 = grouped[x][:, 512 * first : 512 * (first + count)].bitcast(F32)
             if x == "k":
-                g32 = grouped[x][:].bitcast(F32).rearrange("p (b j r u) -> p b j r u", j=P, r=2, u=2)
-                src = live[(x, b)][:].rearrange("p r u j -> p j r u")
+                dst = g32.rearrange("p (j r u) -> p j r u", j=P, u=2)
+                src = live[(x, first)][:].rearrange("p r u j -> p j r u")
             else:
-                g32 = grouped[x][:].bitcast(F32).rearrange("p (b r j u) -> p b r j u", r=2, j=P, u=2)
-                src = live[(x, b)][:].rearrange("p r u j -> p r j u")
+                dst = g32.rearrange("p (r j u) -> p r j u", j=P, u=2)
+                src = live[(x, first)][:].rearrange("p r u j -> p r j u")
             if on_vector:
-                nc.vector.tensor_copy(out=g32[:, b], in_=src)
+                nc.vector.tensor_copy(out=dst, in_=src)
             else:
-                nc.scalar.copy(out=g32[:, b], in_=src)
+                nc.scalar.copy(out=dst, in_=src)
 
-        def quant(x, first, cols):
+        def quant(x, tile, count):
+            first, cols = P * tile, P * count
             nc.vector.quantize_mx(
                 out=codes[x][:, first : first + cols].bitcast(FP8X4),
                 scales=scales[x][:, first : first + cols],
@@ -165,10 +167,13 @@ def tile_sourceawareattention_kernel(tc, q, k, v, s, out):
                     nc.tensor.transpose(et[:, c, h, :], e_words[:, i, w : w + P], ident_f[:])
             live[("et", i)] = et
 
-        def evac_e(i):
+        def evac_e(i, on_vector):
             src = live[("et", i)][:].rearrange("p c h j -> p c j h")
             dst = eg32[:, i]
-            nc.scalar.copy(out=dst, in_=src)
+            if on_vector:
+                nc.vector.tensor_copy(out=dst, in_=src)
+            else:
+                nc.scalar.copy(out=dst, in_=src)
 
         def quant_e(i):
             nc.vector.quantize_mx(
@@ -224,39 +229,42 @@ def tile_sourceawareattention_kernel(tc, q, k, v, s, out):
         def reciprocals(i, n):
             nc.vector.reciprocal(out=rinv[:, i : i + n], in_=rs[:, i : i + n])
 
-        turn("q", 0, 4)
-        evac("q", 0, True)
+        turn("q", 0, 1, 4)
+        evac("q", 0, 1, True)
         for b in range(4):
-            turn("k", b, (5, 6, 7, 4)[b])
-            evac("k", b, b == 1)
+            turn("k", 2 * b, 2, (5, 6, 7, 4)[b])
+            evac("k", 2 * b, 2, b == 1)
             if b == 1:
-                quant("q", 0, 256)
+                quant("q", 0, 1)
             if b >= 1:
-                quant("k", 256 * (b - 1), 256)
-        quant("k", 768, 256)
-        turn("q", 1, 5)
-        evac("q", 1, False)
+                quant("k", 2 * b - 2, 2)
+        quant("k", 6, 2)
+        turn("q", 1, 1, 5)
+        evac("q", 1, 1, False)
+        turn("q", 2, 2, 6)
+        evac("q", 2, 2, False)
         scores(0)
-        scores(1)
-        turn("q", 2, 6)
-        turn("q", 3, 7)
         half_max(0, 0)
+        quant("q", 1, 1)
+        turn("q", 4, 2, 7)
+        evac("q", 4, 2, False)
+        turn("q", 6, 2, 6)
+        evac("q", 6, 2, False)
+        scores(1)
         half_max(0, 1)
-        quant("q", 256, 256)
+        quant("q", 2, 2)
         neg_max(0)
         scores(2)
         exps(0)
-        evac("q", 2, False)
-        evac("q", 3, False)
-        scores(3)
         half_max(1, 0)
         half_max(1, 1)
-        half_max(2, 0)
+        quant("q", 4, 2)
         neg_max(1)
+        scores(3)
+        half_max(2, 0)
         half_max(2, 1)
-        quant("q", 512, 256)
+        quant("q", 6, 2)
         neg_max(2)
-        quant("q", 768, 256)
         half_max(3, 0)
         half_max(3, 1)
         for c in range(2):
@@ -281,17 +289,17 @@ def tile_sourceawareattention_kernel(tc, q, k, v, s, out):
                 row_sums(0, 4)
             else:
                 for i in (2 * p - 2, 2 * p - 1):
-                    evac_e(i)
+                    evac_e(i, i in (2,))
                 for i in (2 * p - 2, 2 * p - 1):
                     if i >= F_LAG:
                         finish(i - F_LAG)
+                    if i == 4:
+                        row_sums(4, 4)
                     quant_e(i)
                     if i == 0:
                         quant_s(1)
                         reciprocals(0, 4)
                     if i == 5:
-                        row_sums(4, 4)
-                    if i == 6:
                         reciprocals(4, 4)
                 for i in (2 * p - 2, 2 * p - 1):
                     weigh(i)

@@ -196,16 +196,18 @@ def tile_sourceawareattention_kernel(tc, q, k, v, s, out):
                 )
             live[("o", i)] = o_ps
 
-        def finish(i):
-            nc.vector.scalar_tensor_tensor(
-                out=res[:, i, :],
-                in0=live[("o", i)][:],
-                scalar=rinv[:, i : i + 1],
-                in1=v_sb[:, i, :],
-                op0=ALU.mult,
-                op1=ALU.mult,
-            )
-            nc.sync.dma_start(out=o_view[:, i, :], in_=res[:, i, :])
+        def finish(i, parts=1):
+            w = D // parts
+            for d in range(0, D, w):
+                nc.vector.scalar_tensor_tensor(
+                    out=res[:, i, d : d + w],
+                    in0=live[("o", i)][:, d : d + w],
+                    scalar=rinv[:, i : i + 1],
+                    in1=v_sb[:, i, d : d + w],
+                    op0=ALU.mult,
+                    op1=ALU.mult,
+                )
+                nc.sync.dma_start(out=o_view[:, i, d : d + w], in_=res[:, i, d : d + w])
 
         def group_s(c):
             for h in (1, 0):
@@ -259,13 +261,13 @@ def tile_sourceawareattention_kernel(tc, q, k, v, s, out):
         half_max(1, 0)
         half_max(1, 1)
         quant("q", 4, 2)
+        quant("q", 6, 2)
         neg_max(1)
         scores(3)
         half_max(2, 0)
         half_max(2, 1)
-        quant("q", 6, 2)
-        neg_max(2)
         half_max(3, 0)
+        neg_max(2)
         half_max(3, 1)
         for c in range(2):
             group_s(c)
@@ -288,6 +290,8 @@ def tile_sourceawareattention_kernel(tc, q, k, v, s, out):
                 neg_max(7)
                 row_sums(0, 4)
             else:
+                if p > 1:
+                    weigh(2 * p - 3)
                 for i in (2 * p - 2, 2 * p - 1):
                     evac_e(i, i in (2,))
                 for i in (2 * p - 2, 2 * p - 1):
@@ -301,7 +305,8 @@ def tile_sourceawareattention_kernel(tc, q, k, v, s, out):
                         reciprocals(0, 4)
                     if i == 5:
                         reciprocals(4, 4)
-                for i in (2 * p - 2, 2 * p - 1):
-                    weigh(i)
-        for i in range(NT - F_LAG, NT):
-            finish(i)
+                weigh(2 * p - 2)
+        weigh(7)
+        finish(5)
+        finish(6)
+        finish(7, 2)

@@ -59,6 +59,8 @@ def tile_sourceawareattention_kernel(tc, q, k, v, s, out):
         make_identity(nc, ident_f[:])
         warm_in = keep.tile([P, 1], F32, name="warm_in")
         warm_out = keep.tile([P, 1], F32, name="warm_out")
+        zero = keep.tile([P, 512], BF16, name="zero")
+        nc.vector.memset(zero[:], 0.0)
         nc.vector.memset(warm_in[:], 0.0)
         nc.scalar.activation(out=warm_out[:], in_=warm_in[:], func=ACT.Exp)
 
@@ -119,6 +121,10 @@ def tile_sourceawareattention_kernel(tc, q, k, v, s, out):
                 scales=scales[x][:, first : first + cols],
                 in_=grouped[x][:, 4 * first : 4 * (first + cols)],
             )
+
+        def busy(n, cols):
+            w = bank(n, [P, 512], F32)
+            nc.tensor.matmul(w[:, 0:cols], lhsT=zero[:, 0:P], rhs=zero[:, 0:cols], start=True, stop=True)
 
         def scores(i):
             for n in range(2):
@@ -231,11 +237,14 @@ def tile_sourceawareattention_kernel(tc, q, k, v, s, out):
         def reciprocals(i, n):
             nc.vector.reciprocal(out=rinv[:, i : i + n], in_=rs[:, i : i + n])
 
+        for n in range(3):
+            busy(n, 512)
         turn("q", 0, 1, 4)
         evac("q", 0, 1, True)
         for b in range(4):
             turn("k", 2 * b, 2, (5, 6, 7, 4)[b])
             evac("k", 2 * b, 2, b == 1)
+            busy(b, 320)
             if b == 1:
                 quant("q", 0, 1)
             if b >= 1:

@@ -40,6 +40,8 @@ def tile_sourceawareattention_kernel(tc, q, k, v, s, out):
         def bank(n, shape, dtype):
             return psum.tile(shape, dtype, name="bank%d" % n, tag="bank%d" % n)
 
+        zero = keep.tile([P, P], BF16, name="zero")
+        nc.vector.memset(zero[:], 0.0)
         k_sb = keep.tile([P, 2, 4, D], BF16, name="k_sb")
         q_sb = keep.tile([P, NT, D], BF16, name="q_sb")
         s_sb = keep.tile([P, 2, 4, D], BF16, name="s_sb")
@@ -59,8 +61,6 @@ def tile_sourceawareattention_kernel(tc, q, k, v, s, out):
         make_identity(nc, ident_f[:])
         warm_in = keep.tile([P, 1], F32, name="warm_in")
         warm_out = keep.tile([P, 1], F32, name="warm_out")
-        zero = keep.tile([P, 512], BF16, name="zero")
-        nc.vector.memset(zero[:], 0.0)
         nc.vector.memset(warm_in[:], 0.0)
         nc.scalar.activation(out=warm_out[:], in_=warm_in[:], func=ACT.Exp)
 
@@ -122,9 +122,10 @@ def tile_sourceawareattention_kernel(tc, q, k, v, s, out):
                 in_=grouped[x][:, 4 * first : 4 * (first + cols)],
             )
 
-        def busy(n, cols):
-            w = bank(n, [P, 512], F32)
-            nc.tensor.matmul(w[:, 0:cols], lhsT=zero[:, 0:P], rhs=zero[:, 0:cols], start=True, stop=True)
+        def busy(n, count):
+            w = bank(n, [P, 4, P], F32)
+            for j in range(count):
+                nc.tensor.matmul(w[:, j % 4, :], lhsT=zero[:], rhs=zero[:], start=True, stop=True)
 
         def scores(i):
             for n in range(2):
@@ -237,14 +238,14 @@ def tile_sourceawareattention_kernel(tc, q, k, v, s, out):
         def reciprocals(i, n):
             nc.vector.reciprocal(out=rinv[:, i : i + n], in_=rs[:, i : i + n])
 
-        for n in range(3):
-            busy(n, 512)
+        for n in range(4):
+            busy(n, 4)
         turn("q", 0, 1, 4)
         evac("q", 0, 1, True)
         for b in range(4):
             turn("k", 2 * b, 2, (5, 6, 7, 4)[b])
             evac("k", 2 * b, 2, b == 1)
-            busy(b, 320)
+            busy(b, 3)
             if b == 1:
                 quant("q", 0, 1)
             if b >= 1:
@@ -292,8 +293,10 @@ def tile_sourceawareattention_kernel(tc, q, k, v, s, out):
         for p in range(NT // 2 + 1):
             if p < NT // 2:
                 exps(4 + p)
-                turn_e(2 * p)
-                turn_e(2 * p + 1)
+                for i in (2 * p, 2 * p + 1):
+                    if i < 4:
+                        busy(i, 3)
+                    turn_e(i)
             if p == 0:
                 quant_s(0)
                 neg_max(7)

@@ -293,10 +293,8 @@ def tile_sourceawareattention_kernel(tc, q, k, v, s, out):
         for p in range(NT // 2 + 1):
             if p < NT // 2:
                 exps(4 + p)
-                for i in (2 * p, 2 * p + 1):
-                    if i < 4:
-                        busy(i, 3)
-                    turn_e(i)
+                turn_e(2 * p)
+                turn_e(2 * p + 1)
             if p == 0:
                 quant_s(0)
                 neg_max(7)
@@ -317,6 +315,8 @@ def tile_sourceawareattention_kernel(tc, q, k, v, s, out):
                         reciprocals(0, 4)
                     if i == 5:
                         reciprocals(4, 4)
+                if p == 1:
+                    busy(0, 4)
                 weigh(2 * p - 2)
         weigh(7)
         finish(5)

@@ -76,6 +76,7 @@ def tile_sourceawareattention_kernel(tc, q, k, v, s, out):
         eg = keep.tile([P, NT, 2, P, 4], BF16, name="eg", align_bytes=64)
         ec = keep.tile([P, NT, 2 * P], U32, name="ec", align_bytes=64)
         es = keep.tile([P, NT, 2 * P], U8, name="es", align_bytes=64)
+        scaled = keep.tile([P, D], F32, name="scaled")
         res = keep.tile([P, NT, D], F32, name="res")
         mx2 = keep.tile([P, NT, 2], F32, name="mx2")
         nm = keep.tile([P, NT], F32, name="nm")
@@ -215,6 +216,12 @@ def tile_sourceawareattention_kernel(tc, q, k, v, s, out):
                     op1=ALU.mult,
                 )
                 nc.sync.dma_start(out=o_view[:, i, d : d + w], in_=res[:, i, d : d + w])
+        def scale_o(i):
+            nc.scalar.activation(out=scaled[:], in_=live[("o", i)][:], func=ACT.Copy, scale=rinv[:, i : i + 1])
+
+        def times_v(i):
+            nc.gpsimd.tensor_tensor(out=res[:, i, :], in0=scaled[:], in1=v_sb[:, i, :], op=ALU.mult)
+            nc.scalar.dma_start(out=o_view[:, i, :], in_=res[:, i, :])
 
         def group_s(c):
             for h in (1, 0):
@@ -304,12 +311,17 @@ def tile_sourceawareattention_kernel(tc, q, k, v, s, out):
                     weigh(2 * p - 3)
                 for i in (2 * p - 2, 2 * p - 1):
                     evac_e(i, i in (2,))
+                if p == 4:
+                    scale_o(4)
+                    times_v(4)
                 for i in (2 * p - 2, 2 * p - 1):
-                    if i >= F_LAG:
+                    if F_LAG <= i < 6:
                         finish(i - F_LAG)
                     if i == 4:
                         row_sums(4, 4)
                     quant_e(i)
+                    if i == 6:
+                        finish(3)
                     if i == 0:
                         quant_s(1)
                         reciprocals(0, 4)

from contextlib import ExitStack
import math

import concourse.mybir as mybir
from concourse.masks import make_identity

FLOPS = 2 * 2 * 1024 * 1024 * 512

BF16 = mybir.dt.bfloat16
F32 = mybir.dt.float32
U32 = mybir.dt.uint32
U8 = mybir.dt.uint8
FP8X4 = mybir.dt.float8_e4m3fn_x4
ACT = mybir.ActivationFunctionType
ALU = mybir.AluOpType
AX = mybir.AxisListType

P = 128
T = 1024
D = 512
NT = T // P
F_LAG = 3


def tile_sourceawareattention_kernel(tc, q, k, v, s, out):
    nc = tc.nc
    inv_sqrt_d = 1.0 / math.sqrt(D)

    q_view = q.flatten_outer_dims().rearrange("(p i) d -> p i d", i=NT)
    v_view = v.flatten_outer_dims().rearrange("(p i) d -> p i d", i=NT)
    o_view = out.flatten_outer_dims().rearrange("(p i) d -> p i d", i=NT)
    k_view = k.flatten_outer_dims().rearrange("(c p t) d -> p c t d", c=2, t=4)
    s_view = s.flatten_outer_dims().rearrange("(c p t) d -> p c t d", c=2, t=4)

    with ExitStack() as ctx:
        keep = ctx.enter_context(tc.tile_pool(name="keep", bufs=1))
        psum = ctx.enter_context(tc.psum_pool(name="psum", bufs=1))
        ctx.enter_context(tc.manual_schedule())

        def bank(n, shape, dtype):
            return psum.tile(shape, dtype, name="bank%d" % n, tag="bank%d" % n)

        zero = keep.tile([P, P], BF16, name="zero")
        nc.vector.memset(zero[:], 0.0)
        k_sb = keep.tile([P, 2, 4, D], BF16, name="k_sb")
        q_sb = keep.tile([P, NT, D], BF16, name="q_sb")
        s_sb = keep.tile([P, 2, 4, D], BF16, name="s_sb")
        v_sb = keep.tile([P, NT, D], BF16, name="v_sb")
        nc.sync.dma_start(out=q_sb[:, 0:1, :], in_=q_view[:, 0:1, :])
        for c in range(2):
            for h in range(2):
                nc.sync.dma_start(out=k_sb[:, c, 2 * h : 2 * h + 2, :], in_=k_view[:, c, 2 * h : 2 * h + 2, :])
        for i, j in ((1, 4), (4, 8)):
            nc.sync.dma_start(out=q_sb[:, i:j, :], in_=q_view[:, i:j, :])
        for c in range(2):
            nc.sync.dma_start(out=s_sb[:, c], in_=s_view[:, c])
        for h in range(2):
            nc.sync.dma_start(out=v_sb[:, 4 * h : 4 * h + 4, :], in_=v_view[:, 4 * h : 4 * h + 4, :])

        ident_f = keep.tile([P, P], F32, name="ident_f")
        make_identity(nc, ident_f[:])
        warm_in = keep.tile([P, 1], F32, name="warm_in")
        warm_out = keep.tile([P, 1], F32, name="warm_out")
        nc.vector.memset(warm_in[:], 0.0)
        nc.scalar.activation(out=warm_out[:], in_=warm_in[:], func=ACT.Exp)

        kg = keep.tile([P, 4 * T], BF16, name="kg", align_bytes=64)
        qg = keep.tile([P, 4 * T], BF16, name="qg", align_bytes=64)
        kc = keep.tile([P, T], U32, name="kc", align_bytes=64)
        qc = keep.tile([P, T], U32, name="qc", align_bytes=64)
        ks = keep.tile([P, T], U8, name="ks", align_bytes=64)
        qs = keep.tile([P, T], U8, name="qs", align_bytes=64)
        sc = keep.tile([P, 2, D], U32, name="sc", align_bytes=64)
        ss = keep.tile([P, 2, D], U8, name="ss", align_bytes=64)
        e_sb = keep.tile([P, NT, T], BF16, name="e_sb")
        eg = keep.tile([P, NT, 2, P, 4], BF16, name="eg", align_bytes=64)
        ec = keep.tile([P, NT, 2 * P], U32, name="ec", align_bytes=64)
        es = keep.tile([P, NT, 2 * P], U8, name="es", align_bytes=64)
        scaled = keep.tile([P, D], F32, name="scaled")
        res = keep.tile([P, NT, D], F32, name="res")
        mx2 = keep.tile([P, NT, 2], F32, name="mx2")
        nm = keep.tile([P, NT], F32, name="nm")
        sums = keep.tile([P, NT, 2], F32, name="sums")
        rs = keep.tile([P, NT], F32, name="rs")
        rinv = keep.tile([P, NT], F32, name="rinv")

        words = {
            "k": k_sb[:].rearrange("p c t d -> p (c t) d").bitcast(F32),
            "q": q_sb[:].bitcast(F32),
        }
        grouped = {"k": kg, "q": qg}
        codes = {"k": kc, "q": qc}
        scales = {"k": ks, "q": qs}
        eg32 = eg[:].rearrange("p i c j t -> p i c (j t)").bitcast(F32).rearrange("p i c (j h) -> p i c j h", h=2)
        live = {}
        sg = [qg[:, 2048 * (1 - c) : 2048 * (1 - c) + 2048].rearrange("p (d t) -> p d t", t=4) for c in range(2)]

        def turn(x, first, count, n):
            xt = bank(n, [P, count, 2, P], F32)
            for r in range(count):
                for u in range(2):
                    nc.tensor.transpose(xt[:, r, u, :], words[x][:, first + r, P * u : P * u + P], ident_f[:])
            live[(x, first)] = xt

        def evac(x, first, count, on_vector):
            g32 = grouped[x][:, 512 * first : 512 * (first + count)].bitcast(F32)
            if x == "k":
                dst = g32.rearrange("p (j r u) -> p j r u", j=P, u=2)
                src = live[(x, first)][:].rearrange("p r u j -> p j r u")
            else:
                dst = g32.rearrange("p (r j u) -> p r j u", j=P, u=2)
                src = live[(x, first)][:].rearrange("p r u j -> p r j u")
            if on_vector:
                nc.vector.tensor_copy(out=dst, in_=src)
            else:
                nc.scalar.copy(out=dst, in_=src)

        def quant(x, tile, count):
            first, cols = P * tile, P * count
            nc.vector.quantize_mx(
                out=codes[x][:, first : first + cols].bitcast(FP8X4),
                scales=scales[x][:, first : first + cols],
                in_=grouped[x][:, 4 * first : 4 * (first + cols)],
            )

        def busy(n, count):
            w = bank(n, [P, 4, P], F32)
            for j in range(count):
                nc.tensor.matmul(w[:, j % 4, :], lhsT=zero[:], rhs=zero[:], start=True, stop=True)

        def scores(i):
            for n in range(2):
                z = bank((2 * i + n) % 8, [P, 512], F32)
                nc.tensor.matmul_mx(
                    out=z[:],
                    lhsT=qc[:, P * i : P * i + P].bitcast(FP8X4),
                    lhsT_scale=qs[:, P * i : P * i + P],
                    rhs=kc[:, 512 * n : 512 * n + 512].bitcast(FP8X4),
                    rhs_scale=ks[:, 512 * n : 512 * n + 512],
                    start=True,
                    stop=True,
                )
                live[("z", i, n)] = z

        def half_max(i, n):
            nc.vector.tensor_reduce(out=mx2[:, i, n : n + 1], in_=live[("z", i, n)][:], axis=AX.X, op=ALU.max)

        def neg_max(i):
            nc.vector.tensor_scalar(
                out=nm[:, i : i + 1],
                in0=mx2[:, i, 0:1],
                scalar1=mx2[:, i, 1:2],
                scalar2=-inv_sqrt_d,
                op0=ALU.max,
                op1=ALU.mult,
            )

        def exps(i):
            for n in range(2):
                nc.scalar.activation(
                    out=e_sb[:, i, 512 * n : 512 * n + 512],
                    in_=live[("z", i, n)][:],
                    func=ACT.Exp,
                    bias=nm[:, i : i + 1],
                    scale=inv_sqrt_d,
                    accum_out=sums[:, i, n : n + 1],
                )

        def turn_e(i):
            et = bank(i, [P, 2, 2, P], F32)
            e_words = e_sb[:].bitcast(F32)
            for c in range(2):
                for h in range(2):
                    w = 256 * c + P * h
                    nc.tensor.transpose(et[:, c, h, :], e_words[:, i, w : w + P], ident_f[:])
            live[("et", i)] = et

        def evac_e(i, on_vector):
            src = live[("et", i)][:].rearrange("p c h j -> p c j h")
            dst = eg32[:, i]
            if on_vector:
                nc.vector.tensor_copy(out=dst, in_=src)
            else:
                nc.scalar.copy(out=dst, in_=src)

        def quant_e(i):
            nc.vector.quantize_mx(
                out=ec[:, i, :].bitcast(FP8X4),
                scales=es[:, i, :],
                in_=eg[:, i].rearrange("p c j t -> p (c j t)"),
            )

        def weigh(i):
            o_ps = bank(i, [P, D], F32)
            for c in range(2):
                nc.tensor.matmul_mx(
                    out=o_ps[:],
                    lhsT=ec[:, i, P * c : P * c + P].bitcast(FP8X4),
                    lhsT_scale=es[:, i, P * c : P * c + P],
                    rhs=sc[:, c, :].bitcast(FP8X4),
                    rhs_scale=ss[:, c, :],
                    start=(c == 0),
                    stop=(c == 1),
                )
            live[("o", i)] = o_ps

        def finish(i, parts=1):
            w = D // parts
            for d in range(0, D, w):
                nc.vector.scalar_tensor_tensor(
                    out=res[:, i, d : d + w],
                    in0=live[("o", i)][:, d : d + w],
                    scalar=rinv[:, i : i + 1],
                    in1=v_sb[:, i, d : d + w],
                    op0=ALU.mult,
                    op1=ALU.mult,
                )
                nc.sync.dma_start(out=o_view[:, i, d : d + w], in_=res[:, i, d : d + w])
        def scale_o(i):
            nc.scalar.activation(out=scaled[:], in_=live[("o", i)][:], func=ACT.Copy, scale=rinv[:, i : i + 1])

        def times_v(i):
            nc.gpsimd.tensor_tensor(out=res[:, i, :], in0=scaled[:], in1=v_sb[:, i, :], op=ALU.mult)
            nc.scalar.dma_start(out=o_view[:, i, :], in_=res[:, i, :])

        def group_s(c):
            for h in (1, 0):
                nc.gpsimd.tensor_scalar(
                    out=sg[c][:, 256 * h : 256 * h + 256, :],
                    in0=s_sb[:, c, :, 256 * h : 256 * h + 256].rearrange("p t d -> p d t"),
                    scalar1=1.0,
                    scalar2=0.0,
                    op0=ALU.mult,
                    op1=ALU.add,
                )

        def quant_s(c):
            nc.vector.quantize_mx(
                out=sc[:, c, :].bitcast(FP8X4), scales=ss[:, c, :], in_=sg[c].rearrange("p d t -> p (d t)")
            )

        def row_sums(i, n):
            nc.vector.tensor_reduce(out=rs[:, i : i + n], in_=sums[:, i : i + n, :], axis=AX.X, op=ALU.add)

        def reciprocals(i, n):
            nc.vector.reciprocal(out=rinv[:, i : i + n], in_=rs[:, i : i + n])

        for n in range(4):
            busy(n, 4)
        turn("q", 0, 1, 4)
        evac("q", 0, 1, True)
        for b in range(4):
            turn("k", 2 * b, 2, (5, 6, 7, 4)[b])
            evac("k", 2 * b, 2, b == 1)
            busy(b, 3)
            if b == 1:
                quant("q", 0, 1)
            if b >= 1:
                quant("k", 2 * b - 2, 2)
        quant("k", 6, 2)
        turn("q", 1, 1, 5)
        evac("q", 1, 1, False)
        turn("q", 2, 2, 6)
        evac("q", 2, 2, False)
        scores(0)
        half_max(0, 0)
        quant("q", 1, 1)
        turn("q", 4, 2, 7)
        evac("q", 4, 2, False)
        turn("q", 6, 2, 6)
        evac("q", 6, 2, False)
        scores(1)
        half_max(0, 1)
        quant("q", 2, 2)
        neg_max(0)
        scores(2)
        exps(0)
        half_max(1, 0)
        half_max(1, 1)
        quant("q", 4, 2)
        quant("q", 6, 2)
        neg_max(1)
        scores(3)
        half_max(2, 0)
        half_max(2, 1)
        half_max(3, 0)
        neg_max(2)
        half_max(3, 1)
        for c in range(2):
            group_s(c)

        for i in range(NT // 2):
            if i > 0:
                exps(i)
            scores(i + 4)
            half_max(i + 4, 0)
            neg_max(i + 3)
            half_max(i + 4, 1)

        for p in range(NT // 2 + 1):
            if p < NT // 2:
                exps(4 + p)
                turn_e(2 * p)
                turn_e(2 * p + 1)
            if p == 0:
                quant_s(0)
                neg_max(7)
                row_sums(0, 4)
            else:
                if p > 1:
                    weigh(2 * p - 3)
                for i in (2 * p - 2, 2 * p - 1):
                    evac_e(i, i in (2,))
                if p == 4:
                    scale_o(4)
                    times_v(4)
                for i in (2 * p - 2, 2 * p - 1):
                    if F_LAG <= i < 6:
                        finish(i - F_LAG)
                    if i == 4:
                        row_sums(4, 4)
                    quant_e(i)
                    if i == 6:
                        finish(3)
                    if i == 0:
                        quant_s(1)
                        reciprocals(0, 4)
                    if i == 5:
                        reciprocals(4, 4)
                if p == 1:
                    busy(0, 4)
                weigh(2 * p - 2)
        weigh(7)
        finish(5)
        finish(6)
        finish(7, 2)
